import numpy as np
import ml_dtypes


def mxq(x, axis, fmt="e4m3"):
    dtype, down = {"e4m3": (ml_dtypes.float8_e4m3fn, 7), "e5m2": (ml_dtypes.float8_e5m2, 14)}[fmt]
    v = np.moveaxis(np.asarray(x, np.float32).astype(ml_dtypes.bfloat16).astype(np.float64), axis, -1)
    blocks = v.reshape(v.shape[:-1] + (-1, 32))
    amax = np.abs(blocks).max(-1, keepdims=True)
    byte = np.maximum(np.where(amax > 0, np.frexp(amax)[1] - 1 + 127, 0) - down, 1)
    scale = np.exp2(byte - 127.0)
    codes = (blocks / scale).astype(np.float32).astype(dtype).astype(np.float64)
    return np.moveaxis((codes * scale).reshape(v.shape), -1, axis)


WIDE = False


def mx_kscale(k):
    if not WIDE:
        return np.ones(k)
    levels = np.array([10, -10, 5, -5, 0])
    if k % 512:
        return np.exp2(np.random.permutation(np.resize(levels, k // 32))).repeat(32)
    a = np.empty((k // 512, 16))
    for p in range(k // 512):
        a[p, :8] = np.random.permutation(np.resize(levels, 8))
        for g in range(8):
            far = levels[np.abs(levels - a[p, g]) >= 10]
            a[p, g + 8] = far[np.random.randint(len(far))]
    return np.exp2(a.ravel()).repeat(32)


BF16 = ml_dtypes.bfloat16


def bf(x):
    return np.asarray(x, np.float32).astype(BF16)


def f64(x):
    return np.asarray(x).astype(np.float64)


B, T, D, H = 2, 1024, 512, 2048
R = B * T
EPS = 1e-5


def sigmoid(v):
    return 1.0 / (1.0 + np.exp(-v))


def layer_norm(x, g, b):
    mu = x.mean(-1, keepdims=True)
    var = np.square(x - mu).mean(-1, keepdims=True)
    return (x - mu) / np.sqrt(var + EPS) * g + b


def draw0():
    s, t = mx_kscale(D), mx_kscale(D)
    n = np.random.standard_normal
    return {"x": bf(n((B, T, D))), "yt": bf(n((B, T, D)) * 0.5 * t),
            "ln1_g": bf((1.0 + 0.2 * n(D)) * s), "ln1_b": bf(0.3 * n(D) * s),
            "Wq": bf(n((D, D)) * 1.5 / np.sqrt(D) / s[:, None]), "bq": bf(0.3 * n(D)),
            "Wo": bf(n((D, D)) * 2.5 / np.sqrt(D) / t[:, None]), "bo": bf(0.3 * n(D))}


def core(x, yt, ln1_g, ln1_b, Wq, bq, Wo, bo):
    xr = f64(x).reshape(R, D)
    h = layer_norm(xr, f64(ln1_g), f64(ln1_b))
    q = (mxq(h, 1, "e4m3") @ mxq(f64(Wq), 0, "e4m3")) + f64(bq)
    y = sigmoid(q) * f64(yt).reshape(R, D)
    attn = (mxq(y, 1, "e4m3") @ mxq(f64(Wo), 0, "e4m3")) + f64(bo)
    return (attn + xr).reshape(B, T, D)


def e4m3fn_bytes(y):
    return np.clip(np.asarray(y, np.float64), -448.0, 448.0).astype(np.float32).astype(ml_dtypes.float8_e4m3fn).view(np.uint8)


def e4m3fn_values(b):
    return np.asarray(b, np.uint8).view(ml_dtypes.float8_e4m3fn).astype(np.float64)


def setup_inputs():
    d = draw0()
    x0 = np.asarray(d['Wq']).astype(np.float64)
    s = (np.max(np.abs(x0), axis=(1,), keepdims=True) / 448.0).astype(np.float32)
    out = {}
    for k, v in d.items():
        if k == 'Wq':
            out['Wq_bytes'] = e4m3fn_bytes(x0 / s.astype(np.float64))
            out['Wq_scale'] = s
        else:
            out[k] = v
    return out


def reference(x, yt, ln1_g, ln1_b, Wq_bytes, Wq_scale, bq, Wo, bo):
    return core(x, yt, ln1_g, ln1_b, e4m3fn_values(Wq_bytes) * Wq_scale.astype(np.float64), bq, Wo, bo)

@@ -1,0 +1,346 @@
+from contextlib import ExitStack
+
+import concourse.mybir as mybir
+from concourse.masks import make_identity
+
+F32 = mybir.dt.float32
+BF16 = mybir.dt.bfloat16
+U8 = mybir.dt.uint8
+U32 = mybir.dt.uint32
+FP8 = mybir.dt.float8_e4m3fn
+FP8X4 = mybir.dt.float8_e4m3fn_x4
+ACT = mybir.ActivationFunctionType
+ALU = mybir.AluOpType
+
+P = 128
+D = 512
+EPS = 1e-5
+GROUPS = (2, 4, 4, 4, 2)
+FLOPS = 2 * 2 * 2048 * D * D
+
+
+def tile_attentionfreetransformerencoder_pb_kernel(tc, x, yt, ln1_g, ln1_b, Wq_bytes, Wq_scale, bq, Wo, bo, out):
+    nc = tc.nc
+    x2 = x.rearrange("b s d -> (b s) d")
+    yt2 = yt.rearrange("b s d -> (b s) d")
+    out2 = out.rearrange("b s d -> (b s) d")
+    starts = [P * sum(GROUPS[:i]) for i in range(len(GROUPS))]
+    last = len(GROUPS) - 1
+
+    def rows(ap, i):
+        n = GROUPS[i]
+        return ap[starts[i] : starts[i] + P * n, :].rearrange("(p n) d -> p n d", n=n)
+
+    with ExitStack() as ctx:
+        keep = ctx.enter_context(tc.tile_pool(name="keep", bufs=1))
+        work = ctx.enter_context(tc.tile_pool(name="work", bufs=2))
+        zpool = ctx.enter_context(tc.tile_pool(name="zpool", bufs=8))
+        xbpool = ctx.enter_context(tc.tile_pool(name="xbpool", bufs=8))
+        opool = ctx.enter_context(tc.tile_pool(name="opool", bufs=4))
+        psum = ctx.enter_context(tc.psum_pool(name="psum", bufs=2))
+        ctx.enter_context(tc.manual_schedule())
+
+        ws = keep.tile([P, 4], F32, name="ws")
+        gb = keep.tile([P, 4], BF16, name="gb")
+        bb = keep.tile([P, 4], BF16, name="bb")
+        bqb = keep.tile([P, 4], BF16, name="bqb")
+        g32 = keep.tile([P, 4], F32, name="g32")
+        nhalf = keep.tile([P, 4], F32, name="nhalf")
+        ones = keep.tile([P, P], BF16, name="ones")
+        bo_row = keep.tile([P, D], BF16, name="bo_row")
+        bo_all = keep.tile([P, D], F32, name="bo_all")
+        ident = keep.tile([P, P], F32, name="ident")
+        dummy = keep.tile([P, 1], F32, name="dummy")
+        wq_raw = keep.tile([P, 4, D], U8, name="wq_raw")
+        wq_wide = keep.tile([P, 4, D], BF16, name="wq_wide")
+        wq_grp = keep.tile([P, 4 * D], BF16, name="wq_grp", align_bytes=64)
+        wq_c = keep.tile([P, D], U32, name="wq_c", align_bytes=64)
+        wq_s = keep.tile([P, D], U8, name="wq_s", align_bytes=64)
+        wo_raw = keep.tile([P, 4, D], BF16, name="wo_raw")
+        wo_grp = keep.tile([P, D, 4], BF16, name="wo_grp", align_bytes=64)
+        wo_c = keep.tile([P, D], U32, name="wo_c", align_bytes=64)
+        wo_s = keep.tile([P, D], U8, name="wo_s", align_bytes=64)
+        xs = [keep.tile([P, n, D], BF16, name="x%d" % i) for i, n in enumerate(GROUPS)]
+        yts = [keep.tile([P, n * D], BF16, name="yt%d" % i) for i, n in enumerate(GROUPS)]
+        mvs = [keep.tile([P, n, 2], F32, name="mv%d" % i) for i, n in enumerate(GROUPS)]
+        bns = [keep.tile([P, n, 6], F32, name="bn%d" % i) for i, n in enumerate(GROUPS)]
+        ves = [keep.tile([P, n], F32, name="ve%d" % i) for i, n in enumerate(GROUPS)]
+        rss = [keep.tile([P, n], F32, name="rs%d" % i) for i, n in enumerate(GROUPS)]
+
+        nc.sync.dma_start(out=xs[0][:], in_=rows(x2, 0))
+        nc.scalar.dma_start(out=ws[:], in_=Wq_scale.rearrange("(p t) o -> p (t o)", t=4))
+        nc.scalar.dma_start(out=gb[:], in_=ln1_g.rearrange("(p t) -> p t", t=4))
+        nc.scalar.dma_start(out=bb[:], in_=ln1_b.rearrange("(p t) -> p t", t=4))
+        nc.scalar.dma_start(out=bqb[:], in_=bq.rearrange("(p t) -> p t", t=4))
+        nc.vector.memset(dummy[:], 0.0)
+        nc.vector.memset(bo_row[:], 0.0)
+        nc.vector.memset(ones[:], 1.0)
+        nc.vector.memset(nhalf[:], -0.5)
+        nc.scalar.activation(out=dummy[:], in_=dummy[:], func=ACT.Sigmoid)
+        make_identity(nc, ident[:])
+        nc.sync.dma_start(out=wq_raw[:], in_=Wq_bytes.rearrange("(p j) n -> p j n", j=4))
+        nc.sync.dma_start(out=xs[1][:], in_=rows(x2, 1))
+        nc.sync.dma_start(out=bo_row[0:1, :], in_=bo.rearrange("(o d) -> o d", o=1))
+        nc.sync.dma_start(out=yts[0][:], in_=rows(yt2, 0).rearrange("p n d -> p (n d)"))
+        nc.sync.dma_start(out=wo_raw[:], in_=Wo.rearrange("(p j) n -> p j n", j=4))
+        nc.sync.dma_start(out=xs[2][:], in_=rows(x2, 2))
+        for i in range(1, len(GROUPS)):
+            nc.sync.dma_start(out=yts[i][:], in_=rows(yt2, i).rearrange("p n d -> p (n d)"))
+            if i + 2 <= last:
+                nc.sync.dma_start(out=xs[i + 2][:], in_=rows(x2, i + 2))
+
+        zs = {}
+        xbs = {}
+        zts = {}
+        hps, hgs, hcs, hss = {}, {}, {}, {}
+        qps, sgs, ytps, ygs, ycs, yss, ots = {}, {}, {}, {}, {}, {}, {}
+
+        def bn(i, n):
+            nc.vector.bn_stats(out=bns[i][:, n, :], in_=xs[i][:, n, :])
+
+        def aggr(i, n):
+            nc.vector.bn_aggr(out=mvs[i][:, n, :], in_=bns[i][:, n, :])
+
+        def stat_units(i):
+            units = []
+            if i <= last:
+                for n in range(GROUPS[i]):
+                    units.append((bn, i, n))
+                    if n > 0:
+                        units.append((aggr, i, n - 1))
+                units.append((aggr, i, GROUPS[i] - 1))
+            return units
+
+        def take(units, count):
+            for k in range(min(count, len(units))):
+                f, i, n = units.pop(0)
+                f(i, n)
+
+        def rstd(i):
+            nc.gpsimd.tensor_scalar(out=ves[i][:], in0=mvs[i][:, :, 1], scalar1=EPS, scalar2=None, op0=ALU.add)
+            nc.gpsimd.tensor_tensor(out=rss[i][:], in0=ves[i][:], in1=nhalf[:, : GROUPS[i]], op=ALU.pow)
+
+        def norm(i):
+            for n in range(GROUPS[i]):
+                z = zpool.tile([P, 4, P], F32, name="z")
+                nc.gpsimd.tensor_scalar(
+                    out=z[:],
+                    in0=xs[i][:, n, :].rearrange("p (q t) -> p t q", t=4),
+                    scalar1=mvs[i][:, n, 0:1],
+                    scalar2=rss[i][:, n : n + 1],
+                    op0=ALU.subtract,
+                    op1=ALU.mult,
+                )
+                zs[i, n] = z
+
+        def tz(i, t):
+            zt = psum.tile([P, D], F32, name="zt")
+            for n in range(GROUPS[i]):
+                nc.tensor.transpose(zt[:, P * n : P * (n + 1)], zs[i, n][:, t, :], ident[:])
+            zts[i, t] = zt
+
+        def ev(i, t):
+            w = P * GROUPS[i]
+            if t == 0:
+                hp = work.tile([P, 4, D], BF16, name="hp")
+                hps[i] = hp
+            nc.scalar.activation(
+                out=hps[i][:, t, :w], in_=zts[i, t][:, :w], func=ACT.Identity, scale=g32[:, t : t + 1], bias=bb[:, t : t + 1]
+            )
+
+        def tz_ev(i):
+            tz(i, 0)
+            tz(i, 1)
+            ev(i, 0)
+            tz(i, 2)
+            ev(i, 1)
+            tz(i, 3)
+            ev(i, 2)
+            ev(i, 3)
+
+        def inter(i):
+            w = P * GROUPS[i]
+            hg = work.tile([P, D, 4], BF16, name="hg", align_bytes=64)
+            hgs[i] = hg
+            nc.scalar.copy(
+                out=hg[:, :w, :].rearrange("p (c i) t -> p c t i", i=4),
+                in_=hps[i][:, :, :w].rearrange("p t (c i) -> p c t i", i=4),
+            )
+
+        def qh(i):
+            w = P * GROUPS[i]
+            hc = work.tile([P, D], U32, name="hc", align_bytes=64)
+            hs = work.tile([P, D], U8, name="hs", align_bytes=64)
+            hcs[i], hss[i] = hc, hs
+            nc.vector.quantize_mx(
+                out=hc[:, :w].bitcast(FP8X4), scales=hs[:, :w], in_=hgs[i][:, :w, :].rearrange("p k t -> p (k t)")
+            )
+
+        def mx1(i, t):
+            w = P * GROUPS[i]
+            qp = psum.tile([P, D], F32, name="qp")
+            qps[i, t] = qp
+            nc.tensor.matmul_mx(
+                out=qp[:, :w],
+                lhsT=wq_c[:, P * t : P * (t + 1)].bitcast(FP8X4),
+                lhsT_scale=wq_s[:, P * t : P * (t + 1)],
+                rhs=hcs[i][:, :w].bitcast(FP8X4),
+                rhs_scale=hss[i][:, :w],
+                start=True,
+                stop=True,
+            )
+
+        def sig(i, t):
+            w = P * GROUPS[i]
+            if t == 0:
+                sg = work.tile([P, 4, D], F32, name="sg")
+                sgs[i] = sg
+            nc.scalar.activation(out=sgs[i][:, t, :w], in_=qps[i, t][:, :w], func=ACT.Sigmoid, bias=bqb[:, t : t + 1])
+
+        def tyt(i, h):
+            ytp = psum.tile([P, D], F32, name="ytp")
+            ytps[i, h] = ytp
+            words = yts[i][:].bitcast(F32)
+            for j in range(2):
+                for u in range(2):
+                    c0 = 256 * (2 * h + j)
+                    nc.tensor.transpose(
+                        ytp[:, 256 * u + P * j : 256 * u + P * (j + 1)], words[:, c0 + u : c0 + 256 : 2], ident[:]
+                    )
+
+        def gate(i, h):
+            if h == 0:
+                yg = work.tile([P, D, 4], BF16, name="yg", align_bytes=64)
+                ygs[i] = yg
+            cols = slice(256 * h, 256 * (h + 1))
+            nc.vector.tensor_tensor(
+                out=ygs[i][:, cols, :].rearrange("p k (u e) -> p k u e", e=2),
+                in0=sgs[i][:, :, cols].rearrange("p (u e) k -> p k u e", e=2),
+                in1=ytps[i, h][:].bitcast(BF16).rearrange("p (u k e) -> p k u e", u=2, e=2),
+                op=ALU.mult,
+            )
+
+        def qy(i, h):
+            if h == 0:
+                yc = work.tile([P, D], U32, name="yc", align_bytes=64)
+                ys = work.tile([P, D], U8, name="ys", align_bytes=64)
+                ycs[i], yss[i] = yc, ys
+            cols = slice(256 * h, 256 * (h + 1))
+            nc.vector.quantize_mx(
+                out=ycs[i][:, cols].bitcast(FP8X4),
+                scales=yss[i][:, cols],
+                in_=ygs[i][:, cols, :].rearrange("p k t -> p (k t)"),
+            )
+
+        def add_bo(i, n):
+            xb = xbpool.tile([P, D], F32, name="xb")
+            xbs[i, n] = xb
+            nc.gpsimd.tensor_tensor(out=xb[:], in0=xs[i][:, n, :], in1=bo_all[:], op=ALU.add)
+
+        def mx2_out(i, n):
+            op = psum.tile([P, D], F32, name="op")
+            nc.tensor.matmul_mx(
+                out=op[:],
+                lhsT=ycs[i][:, P * n : P * (n + 1)].bitcast(FP8X4),
+                lhsT_scale=yss[i][:, P * n : P * (n + 1)],
+                rhs=wo_c[:].bitcast(FP8X4),
+                rhs_scale=wo_s[:],
+                start=True,
+                stop=True,
+            )
+            if n % 2 == 0:
+                ot = opool.tile([P, 2, D], F32, name="ot")
+                ots[i] = ot
+            nc.vector.tensor_tensor(out=ots[i][:, n % 2, :], in0=op[:], in1=xbs[i, n][:], op=ALU.add)
+            if i == last:
+                nc.sync.dma_start(out=rows(out2, i)[:, n, :], in_=ots[i][:, n % 2, :])
+            elif n % 2 == 1:
+                nc.sync.dma_start(out=rows(out2, i)[:, n - 1 : n + 1, :], in_=ots[i][:])
+
+        units = stat_units(0)
+        take(units, 99)
+        rstd(0)
+        norm(0)
+        nc.scalar.copy(out=g32[:], in_=gb[:])
+        for j in range(4):
+            nc.scalar.activation(out=wq_wide[:, j, :], in_=wq_raw[:, j, :].bitcast(FP8), func=ACT.Copy, scale=ws[:, j : j + 1])
+        units = stat_units(1)
+        take(units, 99)
+        bop = psum.tile([P, D], F32, name="bop", tag="op")
+        nc.tensor.matmul(out=bop[:], lhsT=ones[:], rhs=bo_row[:], start=True, stop=True)
+        tz_ev(0)
+        nc.scalar.copy(out=bo_all[:], in_=bop[:])
+        inter(0)
+        nc.vector.tensor_copy(
+            out=wq_grp[:].rearrange("p (t m j) -> p t m j", t=4, j=4),
+            in_=wq_wide[:].rearrange("p j (m t) -> p t m j", t=4),
+        )
+        for n in range(GROUPS[0]):
+            add_bo(0, n)
+        rstd(1)
+        norm(1)
+        nc.vector.quantize_mx(out=wq_c[:].bitcast(FP8X4), scales=wq_s[:], in_=wq_grp[:])
+        qh(0)
+        nc.gpsimd.tensor_scalar(
+            out=wo_grp[:], in0=wo_raw[:].rearrange("p j n -> p n j"), scalar1=1.0, scalar2=0.0, op0=ALU.mult, op1=ALU.add
+        )
+
+        def sig_chain(s):
+            sig(s, 0)
+            mx1(s, 2)
+            sig(s, 1)
+            mx1(s, 3)
+            sig(s, 2)
+            sig(s, 3)
+
+        units = stat_units(2)
+        tyt(0, 0)
+        mx1(0, 0)
+        mx1(0, 1)
+        sig_chain(0)
+        take(units, 99)
+        tz_ev(1)
+        inter(1)
+        gate(0, 0)
+        nc.vector.quantize_mx(out=wo_c[:].bitcast(FP8X4), scales=wo_s[:], in_=wo_grp[:].rearrange("p n j -> p (n j)"))
+        qy(0, 0)
+        rstd(2)
+        norm(2)
+        mx2_out(0, 0)
+        mx2_out(0, 1)
+        qh(1)
+
+        for s in range(1, last + 2):
+            units = stat_units(s + 2)
+            prev = s - 1
+            if prev >= 1:
+                for h in range(GROUPS[prev] // 2):
+                    gate(prev, h)
+            if s + 1 <= last:
+                tz_ev(s + 1)
+                inter(s + 1)
+            if s <= last:
+                for h in range(GROUPS[s] // 2):
+                    tyt(s, h)
+            if prev >= 1:
+                for h in range(GROUPS[prev] // 2):
+                    qy(prev, h)
+                    take(units, 2)
+            if s <= last:
+                mx1(s, 0)
+                mx1(s, 1)
+            if prev >= 1:
+                for n in range(GROUPS[prev]):
+                    mx2_out(prev, n)
+                    take(units, 2)
+            take(units, 99)
+            if s + 2 <= last:
+                rstd(s + 2)
+                norm(s + 2)
+            if s <= last:
+                for n in range(GROUPS[s]):
+                    add_bo(s, n)
+            if s + 1 <= last:
+                qh(s + 1)
+            if s <= last:
+                sig_chain(s)

@@ -15,7 +15,11 @@ ALU = mybir.AluOpType
 P = 128
 D = 512
 EPS = 1e-5
-GROUPS = (2, 4, 4, 4, 2)
+W = 256
+PAIRS = 8
+STEP = [["ev",-1],["rstd",-4],["qh",0],["sig",1],["norm",-3],["xb",1],["bn1",-5],["tz",-2],["mx2",2],["woa",0],["inter",-1],["gate",1],["res0",2],["wqb",-1],["wqa",-5],["bn0",-5],["mx1",0],["ag",-5],["bom",-4],["wqc",-1],["qy",1],["tyt",0],["res1",2],["wob",1]]
+Z_ON_VECTOR = (1, 0, 0, 0, 0, 0, 0, 0)
+INTER_ON_VECTOR = (0, 1, 1, 0, 0, 1, 1, 0)
 FLOPS = 2 * 2 * 2048 * D * D
 
 
@@ -24,19 +28,13 @@ def tile_attentionfreetransformerencoder_pb_kernel(tc, x, yt, ln1_g, ln1_b, Wq_b
     x2 = x.rearrange("b s d -> (b s) d")
     yt2 = yt.rearrange("b s d -> (b s) d")
     out2 = out.rearrange("b s d -> (b s) d")
-    starts = [P * sum(GROUPS[:i]) for i in range(len(GROUPS))]
-    last = len(GROUPS) - 1
 
     def rows(ap, i):
-        n = GROUPS[i]
-        return ap[starts[i] : starts[i] + P * n, :].rearrange("(p n) d -> p n d", n=n)
+        return ap[W * i : W * (i + 1), :].rearrange("(p n) d -> p n d", n=2)
 
     with ExitStack() as ctx:
         keep = ctx.enter_context(tc.tile_pool(name="keep", bufs=1))
-        work = ctx.enter_context(tc.tile_pool(name="work", bufs=2))
-        zpool = ctx.enter_context(tc.tile_pool(name="zpool", bufs=8))
-        xbpool = ctx.enter_context(tc.tile_pool(name="xbpool", bufs=8))
-        opool = ctx.enter_context(tc.tile_pool(name="opool", bufs=4))
+        work = ctx.enter_context(tc.tile_pool(name="work", bufs=4))
         psum = ctx.enter_context(tc.psum_pool(name="psum", bufs=2))
         ctx.enter_context(tc.manual_schedule())
 
@@ -45,7 +43,7 @@ def tile_attentionfreetransformerencoder_pb_kernel(tc, x, yt, ln1_g, ln1_b, Wq_b
         bb = keep.tile([P, 4], BF16, name="bb")
         bqb = keep.tile([P, 4], BF16, name="bqb")
         g32 = keep.tile([P, 4], F32, name="g32")
-        nhalf = keep.tile([P, 4], F32, name="nhalf")
+        nhalf = keep.tile([P, 2], F32, name="nhalf")
         ones = keep.tile([P, P], BF16, name="ones")
         bo_row = keep.tile([P, D], BF16, name="bo_row")
         bo_all = keep.tile([P, D], F32, name="bo_all")
@@ -60,287 +58,235 @@ def tile_attentionfreetransformerencoder_pb_kernel(tc, x, yt, ln1_g, ln1_b, Wq_b
         wo_grp = keep.tile([P, D, 4], BF16, name="wo_grp", align_bytes=64)
         wo_c = keep.tile([P, D], U32, name="wo_c", align_bytes=64)
         wo_s = keep.tile([P, D], U8, name="wo_s", align_bytes=64)
-        xs = [keep.tile([P, n, D], BF16, name="x%d" % i) for i, n in enumerate(GROUPS)]
-        yts = [keep.tile([P, n * D], BF16, name="yt%d" % i) for i, n in enumerate(GROUPS)]
-        mvs = [keep.tile([P, n, 2], F32, name="mv%d" % i) for i, n in enumerate(GROUPS)]
-        bns = [keep.tile([P, n, 6], F32, name="bn%d" % i) for i, n in enumerate(GROUPS)]
-        ves = [keep.tile([P, n], F32, name="ve%d" % i) for i, n in enumerate(GROUPS)]
-        rss = [keep.tile([P, n], F32, name="rs%d" % i) for i, n in enumerate(GROUPS)]
+        xs = [keep.tile([P, 2, D], BF16, name="x%d" % i) for i in range(PAIRS)]
+        yts = [keep.tile([P, 2 * D], BF16, name="yt%d" % i) for i in range(PAIRS)]
+        xbs = [keep.tile([P, 2, D], F32, name="xb%d" % i) for i in range(PAIRS)]
+        mvs = [keep.tile([P, 2, 2], F32, name="mv%d" % i) for i in range(PAIRS)]
+        bns = [keep.tile([P, 2, 6], F32, name="bn%d" % i) for i in range(PAIRS)]
+        ves = [keep.tile([P, 2], F32, name="ve%d" % i) for i in range(PAIRS)]
+        rss = [keep.tile([P, 2], F32, name="rs%d" % i) for i in range(PAIRS)]
+        nms = [keep.tile([P, 2], F32, name="nm%d" % i) for i in range(PAIRS)]
+        nrs = [keep.tile([P, 2], F32, name="nr%d" % i) for i in range(PAIRS)]
 
         nc.sync.dma_start(out=xs[0][:], in_=rows(x2, 0))
         nc.scalar.dma_start(out=ws[:], in_=Wq_scale.rearrange("(p t) o -> p (t o)", t=4))
         nc.scalar.dma_start(out=gb[:], in_=ln1_g.rearrange("(p t) -> p t", t=4))
         nc.scalar.dma_start(out=bb[:], in_=ln1_b.rearrange("(p t) -> p t", t=4))
         nc.scalar.dma_start(out=bqb[:], in_=bq.rearrange("(p t) -> p t", t=4))
-        nc.vector.memset(dummy[:], 0.0)
         nc.vector.memset(bo_row[:], 0.0)
+        nc.vector.memset(dummy[:], 0.0)
         nc.vector.memset(ones[:], 1.0)
         nc.vector.memset(nhalf[:], -0.5)
         nc.scalar.activation(out=dummy[:], in_=dummy[:], func=ACT.Sigmoid)
         make_identity(nc, ident[:])
-        nc.sync.dma_start(out=wq_raw[:], in_=Wq_bytes.rearrange("(p j) n -> p j n", j=4))
         nc.sync.dma_start(out=xs[1][:], in_=rows(x2, 1))
+        nc.sync.dma_start(out=wq_raw[:], in_=Wq_bytes.rearrange("(p j) n -> p j n", j=4))
         nc.sync.dma_start(out=bo_row[0:1, :], in_=bo.rearrange("(o d) -> o d", o=1))
-        nc.sync.dma_start(out=yts[0][:], in_=rows(yt2, 0).rearrange("p n d -> p (n d)"))
-        nc.sync.dma_start(out=wo_raw[:], in_=Wo.rearrange("(p j) n -> p j n", j=4))
         nc.sync.dma_start(out=xs[2][:], in_=rows(x2, 2))
-        for i in range(1, len(GROUPS)):
+        nc.sync.dma_start(out=wo_raw[:], in_=Wo.rearrange("(p j) n -> p j n", j=4))
+        nc.sync.dma_start(out=yts[0][:], in_=rows(yt2, 0).rearrange("p n d -> p (n d)"))
+        for i in range(3, PAIRS):
+            nc.sync.dma_start(out=xs[i][:], in_=rows(x2, i))
+            nc.sync.dma_start(out=yts[i - 2][:], in_=rows(yt2, i - 2).rearrange("p n d -> p (n d)"))
+        for i in range(PAIRS - 2, PAIRS):
             nc.sync.dma_start(out=yts[i][:], in_=rows(yt2, i).rearrange("p n d -> p (n d)"))
-            if i + 2 <= last:
-                nc.sync.dma_start(out=xs[i + 2][:], in_=rows(x2, i + 2))
 
-        zs = {}
-        xbs = {}
-        zts = {}
-        hps, hgs, hcs, hss = {}, {}, {}, {}
-        qps, sgs, ytps, ygs, ycs, yss, ots = {}, {}, {}, {}, {}, {}, {}
+        zs, zts, hps, hgs, hcs, hss = {}, {}, {}, {}, {}, {}
+        qps, sgs, ytps, ygs, ycs, yss, ops, ots = {}, {}, {}, {}, {}, {}, {}, {}
 
-        def bn(i, n):
-            nc.vector.bn_stats(out=bns[i][:, n, :], in_=xs[i][:, n, :])
+        def bn0(i):
+            nc.vector.bn_stats(out=bns[i][:, 0, :], in_=xs[i][:, 0, :])
 
-        def aggr(i, n):
-            nc.vector.bn_aggr(out=mvs[i][:, n, :], in_=bns[i][:, n, :])
+        def bn1(i):
+            nc.vector.bn_stats(out=bns[i][:, 1, :], in_=xs[i][:, 1, :])
 
-        def stat_units(i):
-            units = []
-            if i <= last:
-                for n in range(GROUPS[i]):
-                    units.append((bn, i, n))
-                    if n > 0:
-                        units.append((aggr, i, n - 1))
-                units.append((aggr, i, GROUPS[i] - 1))
-            return units
-
-        def take(units, count):
-            for k in range(min(count, len(units))):
-                f, i, n = units.pop(0)
-                f(i, n)
+        def ag(i):
+            for n in range(2):
+                nc.vector.bn_aggr(out=mvs[i][:, n, :], in_=bns[i][:, n, :])
 
         def rstd(i):
             nc.gpsimd.tensor_scalar(out=ves[i][:], in0=mvs[i][:, :, 1], scalar1=EPS, scalar2=None, op0=ALU.add)
-            nc.gpsimd.tensor_tensor(out=rss[i][:], in0=ves[i][:], in1=nhalf[:, : GROUPS[i]], op=ALU.pow)
+            nc.gpsimd.tensor_tensor(out=rss[i][:], in0=ves[i][:], in1=nhalf[:], op=ALU.pow)
+            if not Z_ON_VECTOR[i]:
+                nc.gpsimd.tensor_scalar(out=nrs[i][:], in0=rss[i][:], scalar1=-1.0, scalar2=None, op0=ALU.mult)
+                nc.gpsimd.tensor_tensor(out=nms[i][:], in0=mvs[i][:, :, 0], in1=nrs[i][:], op=ALU.mult)
+
+        def xb(i):
+            for n in range(2):
+                nc.gpsimd.tensor_tensor(out=xbs[i][:, n, :], in0=xs[i][:, n, :], in1=bo_all[:], op=ALU.add)
 
         def norm(i):
-            for n in range(GROUPS[i]):
-                z = zpool.tile([P, 4, P], F32, name="z")
-                nc.gpsimd.tensor_scalar(
-                    out=z[:],
-                    in0=xs[i][:, n, :].rearrange("p (q t) -> p t q", t=4),
-                    scalar1=mvs[i][:, n, 0:1],
-                    scalar2=rss[i][:, n : n + 1],
-                    op0=ALU.subtract,
-                    op1=ALU.mult,
+            z = work.tile([P, 2, 4, P], F32, name="z")
+            zs[i] = z
+            for n in range(2):
+                z_out = z[:, n, :, :].rearrange("p t (c i) -> p c t i", i=4)
+                z_in = xs[i][:, n, :].rearrange("p (c i t) -> p c t i", i=4, t=4)
+                if Z_ON_VECTOR[i]:
+                    nc.vector.tensor_scalar(
+                        out=z_out,
+                        in0=z_in,
+                        scalar1=mvs[i][:, n, 0:1],
+                        scalar2=rss[i][:, n : n + 1],
+                        op0=ALU.subtract,
+                        op1=ALU.mult,
+                    )
+                else:
+                    nc.scalar.activation(
+                        out=z_out, in_=z_in, func=ACT.Identity, scale=rss[i][:, n : n + 1], bias=nms[i][:, n : n + 1]
+                    )
+
+        def tz(i):
+            for v in range(2):
+                zt = psum.tile([P, 2, W], F32, name="zt")
+                zts[i, v] = zt
+                for t in range(2):
+                    for n in range(2):
+                        nc.tensor.transpose(zt[:, t, P * n : P * (n + 1)], zs[i][:, n, 2 * v + t, :], ident[:])
+
+        def ev(i):
+            hp = work.tile([P, 4, W], BF16, name="hp")
+            hps[i] = hp
+            for t in range(4):
+                nc.scalar.activation(
+                    out=hp[:, t, :],
+                    in_=zts[i, t // 2][:, t % 2, :],
+                    func=ACT.Identity,
+                    scale=g32[:, t : t + 1],
+                    bias=bb[:, t : t + 1],
                 )
-                zs[i, n] = z
-
-        def tz(i, t):
-            zt = psum.tile([P, D], F32, name="zt")
-            for n in range(GROUPS[i]):
-                nc.tensor.transpose(zt[:, P * n : P * (n + 1)], zs[i, n][:, t, :], ident[:])
-            zts[i, t] = zt
-
-        def ev(i, t):
-            w = P * GROUPS[i]
-            if t == 0:
-                hp = work.tile([P, 4, D], BF16, name="hp")
-                hps[i] = hp
-            nc.scalar.activation(
-                out=hps[i][:, t, :w], in_=zts[i, t][:, :w], func=ACT.Identity, scale=g32[:, t : t + 1], bias=bb[:, t : t + 1]
-            )
-
-        def tz_ev(i):
-            tz(i, 0)
-            tz(i, 1)
-            ev(i, 0)
-            tz(i, 2)
-            ev(i, 1)
-            tz(i, 3)
-            ev(i, 2)
-            ev(i, 3)
 
         def inter(i):
-            w = P * GROUPS[i]
-            hg = work.tile([P, D, 4], BF16, name="hg", align_bytes=64)
+            hg = work.tile([P, W, 4], BF16, name="hg", align_bytes=64)
             hgs[i] = hg
-            nc.scalar.copy(
-                out=hg[:, :w, :].rearrange("p (c i) t -> p c t i", i=4),
-                in_=hps[i][:, :, :w].rearrange("p t (c i) -> p c t i", i=4),
+            copy = nc.vector.tensor_copy if INTER_ON_VECTOR[i] else nc.scalar.copy
+            copy(
+                out=hg[:].rearrange("p (c i) t -> p c t i", i=4),
+                in_=hps[i][:].rearrange("p t (c i) -> p c t i", i=4),
             )
 
         def qh(i):
-            w = P * GROUPS[i]
-            hc = work.tile([P, D], U32, name="hc", align_bytes=64)
-            hs = work.tile([P, D], U8, name="hs", align_bytes=64)
+            hc = work.tile([P, W], U32, name="hc", align_bytes=64)
+            hs = work.tile([P, W], U8, name="hs", align_bytes=64)
             hcs[i], hss[i] = hc, hs
-            nc.vector.quantize_mx(
-                out=hc[:, :w].bitcast(FP8X4), scales=hs[:, :w], in_=hgs[i][:, :w, :].rearrange("p k t -> p (k t)")
-            )
+            nc.vector.quantize_mx(out=hc[:].bitcast(FP8X4), scales=hs[:], in_=hgs[i][:].rearrange("p k t -> p (k t)"))
 
-        def mx1(i, t):
-            w = P * GROUPS[i]
-            qp = psum.tile([P, D], F32, name="qp")
-            qps[i, t] = qp
-            nc.tensor.matmul_mx(
-                out=qp[:, :w],
-                lhsT=wq_c[:, P * t : P * (t + 1)].bitcast(FP8X4),
-                lhsT_scale=wq_s[:, P * t : P * (t + 1)],
-                rhs=hcs[i][:, :w].bitcast(FP8X4),
-                rhs_scale=hss[i][:, :w],
-                start=True,
-                stop=True,
-            )
-
-        def sig(i, t):
-            w = P * GROUPS[i]
-            if t == 0:
-                sg = work.tile([P, 4, D], F32, name="sg")
-                sgs[i] = sg
-            nc.scalar.activation(out=sgs[i][:, t, :w], in_=qps[i, t][:, :w], func=ACT.Sigmoid, bias=bqb[:, t : t + 1])
-
-        def tyt(i, h):
-            ytp = psum.tile([P, D], F32, name="ytp")
-            ytps[i, h] = ytp
-            words = yts[i][:].bitcast(F32)
-            for j in range(2):
-                for u in range(2):
-                    c0 = 256 * (2 * h + j)
-                    nc.tensor.transpose(
-                        ytp[:, 256 * u + P * j : 256 * u + P * (j + 1)], words[:, c0 + u : c0 + 256 : 2], ident[:]
+        def mx1(i):
+            for v in range(2):
+                qp = psum.tile([P, 2, W], F32, name="qp")
+                qps[i, v] = qp
+                for t in range(2):
+                    c = P * (2 * v + t)
+                    nc.tensor.matmul_mx(
+                        out=qp[:, t, :],
+                        lhsT=wq_c[:, c : c + P].bitcast(FP8X4),
+                        lhsT_scale=wq_s[:, c : c + P],
+                        rhs=hcs[i][:].bitcast(FP8X4),
+                        rhs_scale=hss[i][:],
+                        start=True,
+                        stop=True,
                     )
 
-        def gate(i, h):
-            if h == 0:
-                yg = work.tile([P, D, 4], BF16, name="yg", align_bytes=64)
-                ygs[i] = yg
-            cols = slice(256 * h, 256 * (h + 1))
+        def sig(i):
+            sg = work.tile([P, 4, W], F32, name="sg")
+            sgs[i] = sg
+            for t in range(4):
+                nc.scalar.activation(
+                    out=sg[:, t, :], in_=qps[i, t // 2][:, t % 2, :], func=ACT.Sigmoid, bias=bqb[:, t : t + 1]
+                )
+
+        def tyt(i):
+            ytp = psum.tile([P, D], F32, name="ytp")
+            ytps[i] = ytp
+            words = yts[i][:].bitcast(F32)
+            for n in range(2):
+                for u in range(2):
+                    nc.tensor.transpose(
+                        ytp[:, 256 * u + P * n : 256 * u + P * (n + 1)], words[:, 256 * n + u : 256 * (n + 1) : 2], ident[:]
+                    )
+
+        def gate(i):
+            yg = work.tile([P, W, 4], BF16, name="yg", align_bytes=64)
+            ygs[i] = yg
             nc.vector.tensor_tensor(
-                out=ygs[i][:, cols, :].rearrange("p k (u e) -> p k u e", e=2),
-                in0=sgs[i][:, :, cols].rearrange("p (u e) k -> p k u e", e=2),
-                in1=ytps[i, h][:].bitcast(BF16).rearrange("p (u k e) -> p k u e", u=2, e=2),
+                out=yg[:].rearrange("p k (u e) -> p k u e", e=2),
+                in0=sgs[i][:].rearrange("p (u e) k -> p k u e", e=2),
+                in1=ytps[i][:].bitcast(BF16).rearrange("p (u k e) -> p k u e", u=2, e=2),
                 op=ALU.mult,
             )
 
-        def qy(i, h):
-            if h == 0:
-                yc = work.tile([P, D], U32, name="yc", align_bytes=64)
-                ys = work.tile([P, D], U8, name="ys", align_bytes=64)
-                ycs[i], yss[i] = yc, ys
-            cols = slice(256 * h, 256 * (h + 1))
-            nc.vector.quantize_mx(
-                out=ycs[i][:, cols].bitcast(FP8X4),
-                scales=yss[i][:, cols],
-                in_=ygs[i][:, cols, :].rearrange("p k t -> p (k t)"),
+        def qy(i):
+            yc = work.tile([P, W], U32, name="yc", align_bytes=64)
+            ys = work.tile([P, W], U8, name="ys", align_bytes=64)
+            ycs[i], yss[i] = yc, ys
+            nc.vector.quantize_mx(out=yc[:].bitcast(FP8X4), scales=ys[:], in_=ygs[i][:].rearrange("p k t -> p (k t)"))
+
+        def mx2(i):
+            for n in range(2):
+                op = psum.tile([P, D], F32, name="op")
+                ops[i, n] = op
+                nc.tensor.matmul_mx(
+                    out=op[:],
+                    lhsT=ycs[i][:, P * n : P * (n + 1)].bitcast(FP8X4),
+                    lhsT_scale=yss[i][:, P * n : P * (n + 1)],
+                    rhs=wo_c[:].bitcast(FP8X4),
+                    rhs_scale=wo_s[:],
+                    start=True,
+                    stop=True,
+                )
+
+        def res0(i):
+            ot = work.tile([P, 2, D], F32, name="ot")
+            ots[i] = ot
+            nc.vector.tensor_tensor(out=ot[:, 0, :], in0=ops[i, 0][:], in1=xbs[i][:, 0, :], op=ALU.add)
+            if i == PAIRS - 1:
+                nc.sync.dma_start(out=rows(out2, i)[:, 0, :], in_=ot[:, 0, :])
+
+        def res1(i):
+            nc.vector.tensor_tensor(out=ots[i][:, 1, :], in0=ops[i, 1][:], in1=xbs[i][:, 1, :], op=ALU.add)
+            if i == PAIRS - 1:
+                nc.sync.dma_start(out=rows(out2, i)[:, 1, :], in_=ots[i][:, 1, :])
+            else:
+                nc.sync.dma_start(out=rows(out2, i), in_=ots[i][:])
+
+        def wqa(i):
+            for u in range(4):
+                nc.scalar.activation(
+                    out=wq_wide[:, u, :], in_=wq_raw[:, u, :].bitcast(FP8), func=ACT.Copy, scale=ws[:, u : u + 1]
+                )
+
+        def bom(i):
+            bop = psum.tile([P, D], F32, name="bop", tag="op")
+            nc.tensor.matmul(out=bop[:], lhsT=ones[:], rhs=bo_row[:], start=True, stop=True)
+            nc.scalar.copy(out=g32[:], in_=gb[:])
+            nc.scalar.copy(out=bo_all[:], in_=bop[:])
+
+        def wqb(i):
+            nc.vector.tensor_copy(
+                out=wq_grp[:].rearrange("p (t m j) -> p t m j", t=4, j=4),
+                in_=wq_wide[:].rearrange("p j (m t) -> p t m j", t=4),
             )
 
-        def add_bo(i, n):
-            xb = xbpool.tile([P, D], F32, name="xb")
-            xbs[i, n] = xb
-            nc.gpsimd.tensor_tensor(out=xb[:], in0=xs[i][:, n, :], in1=bo_all[:], op=ALU.add)
+        def wqc(i):
+            nc.vector.quantize_mx(out=wq_c[:].bitcast(FP8X4), scales=wq_s[:], in_=wq_grp[:])
 
-        def mx2_out(i, n):
-            op = psum.tile([P, D], F32, name="op")
-            nc.tensor.matmul_mx(
-                out=op[:],
-                lhsT=ycs[i][:, P * n : P * (n + 1)].bitcast(FP8X4),
-                lhsT_scale=yss[i][:, P * n : P * (n + 1)],
-                rhs=wo_c[:].bitcast(FP8X4),
-                rhs_scale=wo_s[:],
-                start=True,
-                stop=True,
+        def woa(i):
+            nc.vector.tensor_copy(
+                out=wo_grp[:].rearrange("p (c i) j -> p c j i", i=4), in_=wo_raw[:].rearrange("p j (c i) -> p c j i", i=4)
             )
-            if n % 2 == 0:
-                ot = opool.tile([P, 2, D], F32, name="ot")
-                ots[i] = ot
-            nc.vector.tensor_tensor(out=ots[i][:, n % 2, :], in0=op[:], in1=xbs[i, n][:], op=ALU.add)
-            if i == last:
-                nc.sync.dma_start(out=rows(out2, i)[:, n, :], in_=ots[i][:, n % 2, :])
-            elif n % 2 == 1:
-                nc.sync.dma_start(out=rows(out2, i)[:, n - 1 : n + 1, :], in_=ots[i][:])
 
-        units = stat_units(0)
-        take(units, 99)
-        rstd(0)
-        norm(0)
-        nc.scalar.copy(out=g32[:], in_=gb[:])
-        for j in range(4):
-            nc.scalar.activation(out=wq_wide[:, j, :], in_=wq_raw[:, j, :].bitcast(FP8), func=ACT.Copy, scale=ws[:, j : j + 1])
-        units = stat_units(1)
-        take(units, 99)
-        bop = psum.tile([P, D], F32, name="bop", tag="op")
-        nc.tensor.matmul(out=bop[:], lhsT=ones[:], rhs=bo_row[:], start=True, stop=True)
-        tz_ev(0)
-        nc.scalar.copy(out=bo_all[:], in_=bop[:])
-        inter(0)
-        nc.vector.tensor_copy(
-            out=wq_grp[:].rearrange("p (t m j) -> p t m j", t=4, j=4),
-            in_=wq_wide[:].rearrange("p j (m t) -> p t m j", t=4),
-        )
-        for n in range(GROUPS[0]):
-            add_bo(0, n)
-        rstd(1)
-        norm(1)
-        nc.vector.quantize_mx(out=wq_c[:].bitcast(FP8X4), scales=wq_s[:], in_=wq_grp[:])
-        qh(0)
-        nc.gpsimd.tensor_scalar(
-            out=wo_grp[:], in0=wo_raw[:].rearrange("p j n -> p n j"), scalar1=1.0, scalar2=0.0, op0=ALU.mult, op1=ALU.add
-        )
+        def wob(i):
+            nc.vector.quantize_mx(out=wo_c[:].bitcast(FP8X4), scales=wo_s[:], in_=wo_grp[:].rearrange("p n j -> p (n j)"))
 
-        def sig_chain(s):
-            sig(s, 0)
-            mx1(s, 2)
-            sig(s, 1)
-            mx1(s, 3)
-            sig(s, 2)
-            sig(s, 3)
-
-        units = stat_units(2)
-        tyt(0, 0)
-        mx1(0, 0)
-        mx1(0, 1)
-        sig_chain(0)
-        take(units, 99)
-        tz_ev(1)
-        inter(1)
-        gate(0, 0)
-        nc.vector.quantize_mx(out=wo_c[:].bitcast(FP8X4), scales=wo_s[:], in_=wo_grp[:].rearrange("p n j -> p (n j)"))
-        qy(0, 0)
-        rstd(2)
-        norm(2)
-        mx2_out(0, 0)
-        mx2_out(0, 1)
-        qh(1)
-
-        for s in range(1, last + 2):
-            units = stat_units(s + 2)
-            prev = s - 1
-            if prev >= 1:
-                for h in range(GROUPS[prev] // 2):
-                    gate(prev, h)
-            if s + 1 <= last:
-                tz_ev(s + 1)
-                inter(s + 1)
-            if s <= last:
-                for h in range(GROUPS[s] // 2):
-                    tyt(s, h)
-            if prev >= 1:
-                for h in range(GROUPS[prev] // 2):
-                    qy(prev, h)
-                    take(units, 2)
-            if s <= last:
-                mx1(s, 0)
-                mx1(s, 1)
-            if prev >= 1:
-                for n in range(GROUPS[prev]):
-                    mx2_out(prev, n)
-                    take(units, 2)
-            take(units, 99)
-            if s + 2 <= last:
-                rstd(s + 2)
-                norm(s + 2)
-            if s <= last:
-                for n in range(GROUPS[s]):
-                    add_bo(s, n)
-            if s + 1 <= last:
-                qh(s + 1)
-            if s <= last:
-                sig_chain(s)
+        table = {
+            "bn0": bn0, "bn1": bn1, "ag": ag, "rstd": rstd, "xb": xb, "norm": norm, "tz": tz, "ev": ev, "inter": inter, "qh": qh,
+            "mx1": mx1, "sig": sig, "tyt": tyt, "gate": gate, "qy": qy, "mx2": mx2, "res0": res0, "res1": res1,
+            "wqa": wqa, "bom": bom, "wqb": wqb, "wqc": wqc, "woa": woa, "wob": wob,
+        }
+        once = ("wqa", "bom", "wqb", "wqc", "woa", "wob")
+        for s in range(-8, PAIRS + 8):
+            for name, off in STEP:
+                if name in once:
+                    if s == off:
+                        table[name](0)
+                elif 0 <= s - off < PAIRS:
+                    table[name](s - off)

from contextlib import ExitStack

import concourse.mybir as mybir
from concourse.masks import make_identity

F32 = mybir.dt.float32
BF16 = mybir.dt.bfloat16
U8 = mybir.dt.uint8
U32 = mybir.dt.uint32
FP8 = mybir.dt.float8_e4m3fn
FP8X4 = mybir.dt.float8_e4m3fn_x4
ACT = mybir.ActivationFunctionType
ALU = mybir.AluOpType

P = 128
D = 512
EPS = 1e-5
W = 256
PAIRS = 8
STEP = [["ev",-1],["rstd",-4],["qh",0],["sig",1],["norm",-3],["xb",1],["bn1",-5],["tz",-2],["mx2",2],["woa",0],["inter",-1],["gate",1],["res0",2],["wqb",-1],["wqa",-5],["bn0",-5],["mx1",0],["ag",-5],["bom",-4],["wqc",-1],["qy",1],["tyt",0],["res1",2],["wob",1]]
Z_ON_VECTOR = (1, 0, 0, 0, 0, 0, 0, 0)
INTER_ON_VECTOR = (0, 1, 1, 0, 0, 1, 1, 0)
FLOPS = 2 * 2 * 2048 * D * D


def tile_attentionfreetransformerencoder_pb_kernel(tc, x, yt, ln1_g, ln1_b, Wq_bytes, Wq_scale, bq, Wo, bo, out):
    nc = tc.nc
    x2 = x.rearrange("b s d -> (b s) d")
    yt2 = yt.rearrange("b s d -> (b s) d")
    out2 = out.rearrange("b s d -> (b s) d")

    def rows(ap, i):
        return ap[W * i : W * (i + 1), :].rearrange("(p n) d -> p n d", n=2)

    with ExitStack() as ctx:
        keep = ctx.enter_context(tc.tile_pool(name="keep", bufs=1))
        work = ctx.enter_context(tc.tile_pool(name="work", bufs=4))
        psum = ctx.enter_context(tc.psum_pool(name="psum", bufs=2))
        ctx.enter_context(tc.manual_schedule())

        ws = keep.tile([P, 4], F32, name="ws")
        gb = keep.tile([P, 4], BF16, name="gb")
        bb = keep.tile([P, 4], BF16, name="bb")
        bqb = keep.tile([P, 4], BF16, name="bqb")
        g32 = keep.tile([P, 4], F32, name="g32")
        nhalf = keep.tile([P, 2], F32, name="nhalf")
        ones = keep.tile([P, P], BF16, name="ones")
        bo_row = keep.tile([P, D], BF16, name="bo_row")
        bo_all = keep.tile([P, D], F32, name="bo_all")
        ident = keep.tile([P, P], F32, name="ident")
        dummy = keep.tile([P, 1], F32, name="dummy")
        wq_raw = keep.tile([P, 4, D], U8, name="wq_raw")
        wq_wide = keep.tile([P, 4, D], BF16, name="wq_wide")
        wq_grp = keep.tile([P, 4 * D], BF16, name="wq_grp", align_bytes=64)
        wq_c = keep.tile([P, D], U32, name="wq_c", align_bytes=64)
        wq_s = keep.tile([P, D], U8, name="wq_s", align_bytes=64)
        wo_raw = keep.tile([P, 4, D], BF16, name="wo_raw")
        wo_grp = keep.tile([P, D, 4], BF16, name="wo_grp", align_bytes=64)
        wo_c = keep.tile([P, D], U32, name="wo_c", align_bytes=64)
        wo_s = keep.tile([P, D], U8, name="wo_s", align_bytes=64)
        xs = [keep.tile([P, 2, D], BF16, name="x%d" % i) for i in range(PAIRS)]
        yts = [keep.tile([P, 2 * D], BF16, name="yt%d" % i) for i in range(PAIRS)]
        xbs = [keep.tile([P, 2, D], F32, name="xb%d" % i) for i in range(PAIRS)]
        mvs = [keep.tile([P, 2, 2], F32, name="mv%d" % i) for i in range(PAIRS)]
        bns = [keep.tile([P, 2, 6], F32, name="bn%d" % i) for i in range(PAIRS)]
        ves = [keep.tile([P, 2], F32, name="ve%d" % i) for i in range(PAIRS)]
        rss = [keep.tile([P, 2], F32, name="rs%d" % i) for i in range(PAIRS)]
        nms = [keep.tile([P, 2], F32, name="nm%d" % i) for i in range(PAIRS)]
        nrs = [keep.tile([P, 2], F32, name="nr%d" % i) for i in range(PAIRS)]

        nc.sync.dma_start(out=xs[0][:], in_=rows(x2, 0))
        nc.scalar.dma_start(out=ws[:], in_=Wq_scale.rearrange("(p t) o -> p (t o)", t=4))
        nc.scalar.dma_start(out=gb[:], in_=ln1_g.rearrange("(p t) -> p t", t=4))
        nc.scalar.dma_start(out=bb[:], in_=ln1_b.rearrange("(p t) -> p t", t=4))
        nc.scalar.dma_start(out=bqb[:], in_=bq.rearrange("(p t) -> p t", t=4))
        nc.vector.memset(bo_row[:], 0.0)
        nc.vector.memset(dummy[:], 0.0)
        nc.vector.memset(ones[:], 1.0)
        nc.vector.memset(nhalf[:], -0.5)
        nc.scalar.activation(out=dummy[:], in_=dummy[:], func=ACT.Sigmoid)
        make_identity(nc, ident[:])
        nc.sync.dma_start(out=xs[1][:], in_=rows(x2, 1))
        nc.sync.dma_start(out=wq_raw[:], in_=Wq_bytes.rearrange("(p j) n -> p j n", j=4))
        nc.sync.dma_start(out=bo_row[0:1, :], in_=bo.rearrange("(o d) -> o d", o=1))
        nc.sync.dma_start(out=xs[2][:], in_=rows(x2, 2))
        nc.sync.dma_start(out=wo_raw[:], in_=Wo.rearrange("(p j) n -> p j n", j=4))
        nc.sync.dma_start(out=yts[0][:], in_=rows(yt2, 0).rearrange("p n d -> p (n d)"))
        for i in range(3, PAIRS):
            nc.sync.dma_start(out=xs[i][:], in_=rows(x2, i))
            nc.sync.dma_start(out=yts[i - 2][:], in_=rows(yt2, i - 2).rearrange("p n d -> p (n d)"))
        for i in range(PAIRS - 2, PAIRS):
            nc.sync.dma_start(out=yts[i][:], in_=rows(yt2, i).rearrange("p n d -> p (n d)"))

        zs, zts, hps, hgs, hcs, hss = {}, {}, {}, {}, {}, {}
        qps, sgs, ytps, ygs, ycs, yss, ops, ots = {}, {}, {}, {}, {}, {}, {}, {}

        def bn0(i):
            nc.vector.bn_stats(out=bns[i][:, 0, :], in_=xs[i][:, 0, :])

        def bn1(i):
            nc.vector.bn_stats(out=bns[i][:, 1, :], in_=xs[i][:, 1, :])

        def ag(i):
            for n in range(2):
                nc.vector.bn_aggr(out=mvs[i][:, n, :], in_=bns[i][:, n, :])

        def rstd(i):
            nc.gpsimd.tensor_scalar(out=ves[i][:], in0=mvs[i][:, :, 1], scalar1=EPS, scalar2=None, op0=ALU.add)
            nc.gpsimd.tensor_tensor(out=rss[i][:], in0=ves[i][:], in1=nhalf[:], op=ALU.pow)
            if not Z_ON_VECTOR[i]:
                nc.gpsimd.tensor_scalar(out=nrs[i][:], in0=rss[i][:], scalar1=-1.0, scalar2=None, op0=ALU.mult)
                nc.gpsimd.tensor_tensor(out=nms[i][:], in0=mvs[i][:, :, 0], in1=nrs[i][:], op=ALU.mult)

        def xb(i):
            for n in range(2):
                nc.gpsimd.tensor_tensor(out=xbs[i][:, n, :], in0=xs[i][:, n, :], in1=bo_all[:], op=ALU.add)

        def norm(i):
            z = work.tile([P, 2, 4, P], F32, name="z")
            zs[i] = z
            for n in range(2):
                z_out = z[:, n, :, :].rearrange("p t (c i) -> p c t i", i=4)
                z_in = xs[i][:, n, :].rearrange("p (c i t) -> p c t i", i=4, t=4)
                if Z_ON_VECTOR[i]:
                    nc.vector.tensor_scalar(
                        out=z_out,
                        in0=z_in,
                        scalar1=mvs[i][:, n, 0:1],
                        scalar2=rss[i][:, n : n + 1],
                        op0=ALU.subtract,
                        op1=ALU.mult,
                    )
                else:
                    nc.scalar.activation(
                        out=z_out, in_=z_in, func=ACT.Identity, scale=rss[i][:, n : n + 1], bias=nms[i][:, n : n + 1]
                    )

        def tz(i):
            for v in range(2):
                zt = psum.tile([P, 2, W], F32, name="zt")
                zts[i, v] = zt
                for t in range(2):
                    for n in range(2):
                        nc.tensor.transpose(zt[:, t, P * n : P * (n + 1)], zs[i][:, n, 2 * v + t, :], ident[:])

        def ev(i):
            hp = work.tile([P, 4, W], BF16, name="hp")
            hps[i] = hp
            for t in range(4):
                nc.scalar.activation(
                    out=hp[:, t, :],
                    in_=zts[i, t // 2][:, t % 2, :],
                    func=ACT.Identity,
                    scale=g32[:, t : t + 1],
                    bias=bb[:, t : t + 1],
                )

        def inter(i):
            hg = work.tile([P, W, 4], BF16, name="hg", align_bytes=64)
            hgs[i] = hg
            copy = nc.vector.tensor_copy if INTER_ON_VECTOR[i] else nc.scalar.copy
            copy(
                out=hg[:].rearrange("p (c i) t -> p c t i", i=4),
                in_=hps[i][:].rearrange("p t (c i) -> p c t i", i=4),
            )

        def qh(i):
            hc = work.tile([P, W], U32, name="hc", align_bytes=64)
            hs = work.tile([P, W], U8, name="hs", align_bytes=64)
            hcs[i], hss[i] = hc, hs
            nc.vector.quantize_mx(out=hc[:].bitcast(FP8X4), scales=hs[:], in_=hgs[i][:].rearrange("p k t -> p (k t)"))

        def mx1(i):
            for v in range(2):
                qp = psum.tile([P, 2, W], F32, name="qp")
                qps[i, v] = qp
                for t in range(2):
                    c = P * (2 * v + t)
                    nc.tensor.matmul_mx(
                        out=qp[:, t, :],
                        lhsT=wq_c[:, c : c + P].bitcast(FP8X4),
                        lhsT_scale=wq_s[:, c : c + P],
                        rhs=hcs[i][:].bitcast(FP8X4),
                        rhs_scale=hss[i][:],
                        start=True,
                        stop=True,
                    )

        def sig(i):
            sg = work.tile([P, 4, W], F32, name="sg")
            sgs[i] = sg
            for t in range(4):
                nc.scalar.activation(
                    out=sg[:, t, :], in_=qps[i, t // 2][:, t % 2, :], func=ACT.Sigmoid, bias=bqb[:, t : t + 1]
                )

        def tyt(i):
            ytp = psum.tile([P, D], F32, name="ytp")
            ytps[i] = ytp
            words = yts[i][:].bitcast(F32)
            for n in range(2):
                for u in range(2):
                    nc.tensor.transpose(
                        ytp[:, 256 * u + P * n : 256 * u + P * (n + 1)], words[:, 256 * n + u : 256 * (n + 1) : 2], ident[:]
                    )

        def gate(i):
            yg = work.tile([P, W, 4], BF16, name="yg", align_bytes=64)
            ygs[i] = yg
            nc.vector.tensor_tensor(
                out=yg[:].rearrange("p k (u e) -> p k u e", e=2),
                in0=sgs[i][:].rearrange("p (u e) k -> p k u e", e=2),
                in1=ytps[i][:].bitcast(BF16).rearrange("p (u k e) -> p k u e", u=2, e=2),
                op=ALU.mult,
            )

        def qy(i):
            yc = work.tile([P, W], U32, name="yc", align_bytes=64)
            ys = work.tile([P, W], U8, name="ys", align_bytes=64)
            ycs[i], yss[i] = yc, ys
            nc.vector.quantize_mx(out=yc[:].bitcast(FP8X4), scales=ys[:], in_=ygs[i][:].rearrange("p k t -> p (k t)"))

        def mx2(i):
            for n in range(2):
                op = psum.tile([P, D], F32, name="op")
                ops[i, n] = op
                nc.tensor.matmul_mx(
                    out=op[:],
                    lhsT=ycs[i][:, P * n : P * (n + 1)].bitcast(FP8X4),
                    lhsT_scale=yss[i][:, P * n : P * (n + 1)],
                    rhs=wo_c[:].bitcast(FP8X4),
                    rhs_scale=wo_s[:],
                    start=True,
                    stop=True,
                )

        def res0(i):
            ot = work.tile([P, 2, D], F32, name="ot")
            ots[i] = ot
            nc.vector.tensor_tensor(out=ot[:, 0, :], in0=ops[i, 0][:], in1=xbs[i][:, 0, :], op=ALU.add)
            if i == PAIRS - 1:
                nc.sync.dma_start(out=rows(out2, i)[:, 0, :], in_=ot[:, 0, :])

        def res1(i):
            nc.vector.tensor_tensor(out=ots[i][:, 1, :], in0=ops[i, 1][:], in1=xbs[i][:, 1, :], op=ALU.add)
            if i == PAIRS - 1:
                nc.sync.dma_start(out=rows(out2, i)[:, 1, :], in_=ots[i][:, 1, :])
            else:
                nc.sync.dma_start(out=rows(out2, i), in_=ots[i][:])

        def wqa(i):
            for u in range(4):
                nc.scalar.activation(
                    out=wq_wide[:, u, :], in_=wq_raw[:, u, :].bitcast(FP8), func=ACT.Copy, scale=ws[:, u : u + 1]
                )

        def bom(i):
            bop = psum.tile([P, D], F32, name="bop", tag="op")
            nc.tensor.matmul(out=bop[:], lhsT=ones[:], rhs=bo_row[:], start=True, stop=True)
            nc.scalar.copy(out=g32[:], in_=gb[:])
            nc.scalar.copy(out=bo_all[:], in_=bop[:])

        def wqb(i):
            nc.vector.tensor_copy(
                out=wq_grp[:].rearrange("p (t m j) -> p t m j", t=4, j=4),
                in_=wq_wide[:].rearrange("p j (m t) -> p t m j", t=4),
            )

        def wqc(i):
            nc.vector.quantize_mx(out=wq_c[:].bitcast(FP8X4), scales=wq_s[:], in_=wq_grp[:])

        def woa(i):
            nc.vector.tensor_copy(
                out=wo_grp[:].rearrange("p (c i) j -> p c j i", i=4), in_=wo_raw[:].rearrange("p j (c i) -> p c j i", i=4)
            )

        def wob(i):
            nc.vector.quantize_mx(out=wo_c[:].bitcast(FP8X4), scales=wo_s[:], in_=wo_grp[:].rearrange("p n j -> p (n j)"))

        table = {
            "bn0": bn0, "bn1": bn1, "ag": ag, "rstd": rstd, "xb": xb, "norm": norm, "tz": tz, "ev": ev, "inter": inter, "qh": qh,
            "mx1": mx1, "sig": sig, "tyt": tyt, "gate": gate, "qy": qy, "mx2": mx2, "res0": res0, "res1": res1,
            "wqa": wqa, "bom": bom, "wqb": wqb, "wqc": wqc, "woa": woa, "wob": wob,
        }
        once = ("wqa", "bom", "wqb", "wqc", "woa", "wob")
        for s in range(-8, PAIRS + 8):
            for name, off in STEP:
                if name in once:
                    if s == off:
                        table[name](0)
                elif 0 <= s - off < PAIRS:
                    table[name](s - off)
